import numpy as np
import ml_dtypes


def mxq(x, axis, fmt="e4m3"):
    dtype, down = {"e4m3": (ml_dtypes.float8_e4m3fn, 7), "e5m2": (ml_dtypes.float8_e5m2, 14)}[fmt]
    v = np.moveaxis(np.asarray(x, np.float32).astype(ml_dtypes.bfloat16).astype(np.float64), axis, -1)
    blocks = v.reshape(v.shape[:-1] + (-1, 32))
    amax = np.abs(blocks).max(-1, keepdims=True)
    byte = np.maximum(np.where(amax > 0, np.frexp(amax)[1] - 1 + 127, 0) - down, 1)
    scale = np.exp2(byte - 127.0)
    codes = (blocks / scale).astype(np.float32).astype(dtype).astype(np.float64)
    return np.moveaxis((codes * scale).reshape(v.shape), -1, axis)


WIDE = False


def mx_kscale(k):
    if not WIDE:
        return np.ones(k)
    levels = np.array([20, -20, 10, -10, 0])
    if k % 512:
        return np.exp2(np.random.permutation(np.resize(levels, k // 32))).repeat(32)
    a = np.empty((k // 512, 16))
    for p in range(k // 512):
        a[p, :8] = np.random.permutation(np.resize(levels, 8))
        for g in range(8):
            far = levels[np.abs(levels - a[p, g]) >= 10]
            a[p, g + 8] = far[np.random.randint(len(far))]
    return np.exp2(a.ravel()).repeat(32)


BF16 = ml_dtypes.bfloat16


def bf(x):
    return np.asarray(x, np.float32).astype(BF16)


def f64(x):
    return np.asarray(x).astype(np.float64)


B, H, L, E, QD = 8, 1, 128, 2048, 512


def setup_inputs():
    u = mx_kscale(QD)
    x = bf(np.random.standard_normal((B, H, L, E)))
    Wk0 = bf(np.random.standard_normal((QD, E)) * 0.3 / np.sqrt(E))
    bk = bf(0.1 + 0.1 * np.random.standard_normal(QD))
    Wv0 = bf(np.random.standard_normal((QD, E)) * 0.3 / np.sqrt(E))
    bv = bf(0.1 + 0.1 * np.random.standard_normal(QD))
    g = bf(np.random.standard_normal((B, H, L, QD)) * np.exp2(np.random.randint(-12, 1, (B, H, L, 1))) * 256.0 * u)
    K = f64(x) @ f64(Wk0).T + f64(bk)
    V = f64(x) @ f64(Wv0).T + f64(bv)
    return {"x": x,
            "Wk": bf(f64(Wk0) / u[:, None]),
            "bk": bk,
            "Wv": bf(f64(Wv0) / u[:, None]),
            "bv": bv,
            "K": np.asarray(K, np.float32),
            "V": np.asarray(V, np.float32),
            "grad_out": g}


def reference(x, Wk, bk, Wv, bv, K, V, grad_out):
    g = f64(grad_out)
    dK = g * f64(V)
    dV = g * f64(K)
    a = mxq(dK, 3, "e5m2") @ mxq(f64(Wk), 0, "e4m3")
    c = mxq(dV, 3, "e5m2") @ mxq(f64(Wv), 0, "e4m3")
    return a + c

@@ -1,0 +1,189 @@
+from contextlib import ExitStack
+
+import concourse.mybir as mybir
+from concourse.masks import make_identity
+
+F32 = mybir.dt.float32
+BF16 = mybir.dt.bfloat16
+U32 = mybir.dt.uint32
+U8 = mybir.dt.uint8
+E4M3X4 = mybir.dt.float8_e4m3fn_x4
+E5M2X4 = mybir.dt.float8_e5m2_x4
+
+P = 128
+PACK = 4
+QD = P * PACK
+TOKENS = 1024
+E = 2048
+TILES = TOKENS // P
+TILES_PER_LOAD = 2
+LOADS = TILES // TILES_PER_LOAD
+CHUNK = 512
+GROUP = 1024
+GROUPS = E // GROUP
+CHUNKS_PER_GROUP = GROUP // CHUNK
+CHUNKS = E // CHUNK
+AHEAD = 2
+
+FLOPS = 2 * 2 * TOKENS * QD * E
+BYTES = 2 * QD * E * 2 + 2 * TOKENS * QD * 4 + TOKENS * QD * 2 + TOKENS * E * 4
+
+
+def regrouped(dst, src):
+    return (
+        dst.rearrange("p (c i) t -> p c t i", i=4),
+        src.rearrange("p t (c i) -> p c t i", i=4),
+    )
+
+
+def tile_parallelretention_pa_v_kernel(tc, x, Wk, bk, Wv, bv, K, V, grad_out, out):
+    nc = tc.nc
+    g_rows = grad_out.flatten_outer_dims().rearrange("(p j) k -> p j k", j=TILES)
+    factor_rows = [
+        V.flatten_outer_dims().rearrange("(p j) k -> p j k", j=TILES),
+        K.flatten_outer_dims().rearrange("(p j) k -> p j k", j=TILES),
+    ]
+    out_rows = out.flatten_outer_dims().rearrange("(p j) e -> p j e", j=TILES)
+    weight_rows = [
+        Wk.rearrange("(p u e) c -> u p e c", u=2, e=2),
+        Wv.rearrange("(p u e) c -> u p e c", u=2, e=2),
+    ]
+
+    with ExitStack() as ctx:
+        keep = ctx.enter_context(tc.tile_pool(name="keep", bufs=1))
+        w_stage = ctx.enter_context(tc.tile_pool(name="w_stage", bufs=4))
+        tok_stage = ctx.enter_context(tc.tile_pool(name="tok_stage", bufs=4))
+        psum_t = ctx.enter_context(tc.psum_pool(name="psum_t", bufs=2))
+        psum_acc = ctx.enter_context(tc.psum_pool(name="psum_acc", bufs=6))
+
+        identity = keep.tile([P, P], F32)
+        make_identity(nc, identity[:])
+
+        g_sb = [keep.tile([P, TILES_PER_LOAD, QD], BF16, name="g_sb_%d" % i) for i in range(LOADS)]
+        factor_sb = [keep.tile([P, 2, TILES_PER_LOAD, QD], F32, name="factor_sb_%d" % i) for i in range(LOADS)]
+        w_raw = [
+            [keep.tile([P, PACK, GROUP], BF16, name="w_raw_%d_%d" % (group, m)) for m in range(2)]
+            for group in range(GROUPS)
+        ]
+        w_codes = keep.tile([P, 2, E], U32, align_bytes=64)
+        w_scales = keep.tile([P, 2, E], U8, align_bytes=64)
+        tok_codes = keep.tile([P, TILES, 2, P], U32, align_bytes=64)
+        tok_scales = keep.tile([P, TILES, 2, P], U8, align_bytes=64)
+        out_sb = keep.tile([P, TILES, E], F32)
+
+        def load_tokens(i):
+            js = slice(i * TILES_PER_LOAD, (i + 1) * TILES_PER_LOAD)
+            nc.sync.dma_start(out=g_sb[i][:], in_=g_rows[:, js, :])
+            for m in range(2):
+                nc.sync.dma_start(out=factor_sb[i][:, m, :, :], in_=factor_rows[m][:, js, :])
+
+        def load_weights(group):
+            cols = slice(group * GROUP, (group + 1) * GROUP)
+            for m in range(2):
+                for u in range(2):
+                    nc.sync.dma_start(out=w_raw[group][m][:, 2 * u : 2 * u + 2, :], in_=weight_rows[m][u][:, :, cols])
+
+        def regroup_weight(m, chunk):
+            group = chunk // CHUNKS_PER_GROUP
+            vector_cols = CHUNK // 2 if group == 0 else CHUNK
+            raw = w_raw[group][m]
+            c0 = (chunk % CHUNKS_PER_GROUP) * CHUNK
+            c1 = c0 + vector_cols
+            c2 = c0 + CHUNK
+            w_grouped = w_stage.tile([P, CHUNK, PACK], BF16, align_bytes=64)
+            dst, src = regrouped(w_grouped[:, 0:vector_cols, :], raw[:, :, c0:c1])
+            nc.vector.tensor_copy(out=dst, in_=src)
+            if vector_cols < CHUNK:
+                dst, src = regrouped(w_grouped[:, vector_cols:CHUNK, :], raw[:, :, c1:c2])
+                nc.scalar.copy(out=dst, in_=src)
+            return w_grouped
+
+        def quantise_weight(m, chunk, w_grouped):
+            cols = slice(chunk * CHUNK, (chunk + 1) * CHUNK)
+            nc.vector.quantize_mx(
+                out=w_codes[:, m, cols].bitcast(E4M3X4),
+                scales=w_scales[:, m, cols],
+                in_=w_grouped[:].rearrange("p c t -> p (c t)"),
+            )
+
+        def prepare_weights(pieces):
+            waiting = None
+            for m, chunk in pieces:
+                w_grouped = regroup_weight(m, chunk)
+                if waiting is not None:
+                    quantise_weight(*waiting)
+                waiting = (m, chunk, w_grouped)
+            quantise_weight(*waiting)
+
+        def transpose_tokens(j):
+            grads = tok_stage.tile([P, 2, QD], BF16)
+            nc.vector.tensor_tensor(
+                out=grads[:],
+                in0=g_sb[j // TILES_PER_LOAD][:, j % TILES_PER_LOAD, :].unsqueeze(1).to_broadcast([P, 2, QD]),
+                in1=factor_sb[j // TILES_PER_LOAD][:, :, j % TILES_PER_LOAD, :],
+                op=mybir.AluOpType.mult,
+            )
+            grad_words = grads[:].rearrange("p m k -> p (m k)").bitcast(F32)
+            words_t = psum_t.tile([P, 2, 2, P], F32)
+            for m in range(2):
+                for u in range(2):
+                    first = 2 * m * P + u
+                    last = 2 * (m + 1) * P
+                    nc.tensor.transpose(words_t[:, m, u, :], grad_words[:, first:last:2], identity[:])
+            tok_grouped = tok_stage.tile([P, 2 * P * PACK], BF16, align_bytes=64)
+            nc.scalar.copy(
+                out=tok_grouped[:].bitcast(F32).rearrange("p (m r u) -> p m r u", m=2, u=2),
+                in_=words_t[:].rearrange("p m u r -> p m r u"),
+            )
+            return tok_grouped
+
+        def quantise_tokens(j, tok_grouped):
+            nc.vector.quantize_mx(
+                out=tok_codes[:, j, :, :].rearrange("p m r -> p (m r)").bitcast(E5M2X4),
+                scales=tok_scales[:, j, :, :].rearrange("p m r -> p (m r)"),
+                in_=tok_grouped[:],
+            )
+
+        def multiply(j, chunks):
+            for chunk in chunks:
+                cols = slice(chunk * CHUNK, (chunk + 1) * CHUNK)
+                acc = psum_acc.tile([P, CHUNK], F32)
+                for m in range(2):
+                    nc.tensor.matmul_mx(
+                        out=acc[:],
+                        lhsT=tok_codes[:, j, m, :].bitcast(E5M2X4),
+                        lhsT_scale=tok_scales[:, j, m, :],
+                        rhs=w_codes[:, m, cols].bitcast(E4M3X4),
+                        rhs_scale=w_scales[:, m, cols],
+                        start=(m == 0),
+                        stop=(m == 1),
+                    )
+                if chunk == CHUNKS - 1 and j % 2 == 1:
+                    nc.vector.tensor_copy(out=out_sb[:, j, cols], in_=acc[:])
+                else:
+                    nc.scalar.copy(out=out_sb[:, j, cols], in_=acc[:])
+            cols = slice(chunks[0] * CHUNK, (chunks[-1] + 1) * CHUNK)
+            nc.sync.dma_start(out=out_rows[:, j, cols], in_=out_sb[:, j, cols])
+
+        load_tokens(0)
+        load_weights(0)
+        for i in range(1, LOADS):
+            load_tokens(i)
+        for group in range(1, GROUPS):
+            load_weights(group)
+
+        first_chunks = list(range(CHUNKS_PER_GROUP))
+        tok_grouped = [transpose_tokens(j) for j in range(AHEAD)]
+        prepare_weights([(0, chunk) for chunk in first_chunks])
+        quantise_tokens(0, tok_grouped[0])
+        prepare_weights([(1, chunk) for chunk in first_chunks])
+        for j in range(TILES):
+            multiply(j, first_chunks)
+            if j + AHEAD < TILES:
+                tok_grouped.append(transpose_tokens(j + AHEAD))
+            if j + 1 < TILES:
+                quantise_tokens(j + 1, tok_grouped[j + 1])
+        for chunk in range(CHUNKS_PER_GROUP, CHUNKS):
+            prepare_weights([(m, chunk) for m in range(2)])
+            for j in range(TILES):
+                multiply(j, [chunk])

@@ -45,8 +45,8 @@ def tile_parallelretention_pa_v_kernel(tc, x, Wk, bk, Wv, bv, K, V, grad_out, ou
     ]
     out_rows = out.flatten_outer_dims().rearrange("(p j) e -> p j e", j=TILES)
     weight_rows = [
-        Wk.rearrange("(p u e) c -> u p e c", u=2, e=2),
-        Wv.rearrange("(p u e) c -> u p e c", u=2, e=2),
+        Wk.rearrange("(p t) c -> p t c", t=PACK),
+        Wv.rearrange("(p t) c -> p t c", t=PACK),
     ]
 
     with ExitStack() as ctx:
@@ -80,8 +80,7 @@ def tile_parallelretention_pa_v_kernel(tc, x, Wk, bk, Wv, bv, K, V, grad_out, ou
         def load_weights(group):
             cols = slice(group * GROUP, (group + 1) * GROUP)
             for m in range(2):
-                for u in range(2):
-                    nc.sync.dma_start(out=w_raw[group][m][:, 2 * u : 2 * u + 2, :], in_=weight_rows[m][u][:, :, cols])
+                nc.sync.dma_start(out=w_raw[group][m][:], in_=weight_rows[m][:, :, cols])
 
         def regroup_weight(m, chunk):
             group = chunk // CHUNKS_PER_GROUP

@@ -23,6 +23,9 @@ GROUP = 1024
 GROUPS = E // GROUP
 CHUNKS_PER_GROUP = GROUP // CHUNK
 CHUNKS = E // CHUNK
+FIRST_GROUP_VECTOR_COLS = 320
+BY_CHUNK = 6
+SINGLE = 4
 AHEAD = 2
 
 FLOPS = 2 * 2 * TOKENS * QD * E
@@ -60,7 +63,10 @@ def tile_parallelretention_pa_v_kernel(tc, x, Wk, bk, Wv, bv, K, V, grad_out, ou
         make_identity(nc, identity[:])
 
         g_sb = [keep.tile([P, TILES_PER_LOAD, QD], BF16, name="g_sb_%d" % i) for i in range(LOADS)]
-        factor_sb = [keep.tile([P, 2, TILES_PER_LOAD, QD], F32, name="factor_sb_%d" % i) for i in range(LOADS)]
+        factor_sb = [
+            [keep.tile([P, TILES_PER_LOAD, QD], F32, name="factor_sb_%d_%d" % (i, m)) for m in range(2)]
+            for i in range(LOADS)
+        ]
         w_raw = [
             [keep.tile([P, PACK, GROUP], BF16, name="w_raw_%d_%d" % (group, m)) for m in range(2)]
             for group in range(GROUPS)
@@ -75,7 +81,7 @@ def tile_parallelretention_pa_v_kernel(tc, x, Wk, bk, Wv, bv, K, V, grad_out, ou
             js = slice(i * TILES_PER_LOAD, (i + 1) * TILES_PER_LOAD)
             nc.sync.dma_start(out=g_sb[i][:], in_=g_rows[:, js, :])
             for m in range(2):
-                nc.sync.dma_start(out=factor_sb[i][:, m, :, :], in_=factor_rows[m][:, js, :])
+                nc.sync.dma_start(out=factor_sb[i][m][:], in_=factor_rows[m][:, js, :])
 
         def load_weights(group):
             cols = slice(group * GROUP, (group + 1) * GROUP)
@@ -84,7 +90,7 @@ def tile_parallelretention_pa_v_kernel(tc, x, Wk, bk, Wv, bv, K, V, grad_out, ou
 
         def regroup_weight(m, chunk):
             group = chunk // CHUNKS_PER_GROUP
-            vector_cols = CHUNK // 2 if group == 0 else CHUNK
+            vector_cols = FIRST_GROUP_VECTOR_COLS if group == 0 else CHUNK
             raw = w_raw[group][m]
             c0 = (chunk % CHUNKS_PER_GROUP) * CHUNK
             c1 = c0 + vector_cols
@@ -115,20 +121,21 @@ def tile_parallelretention_pa_v_kernel(tc, x, Wk, bk, Wv, bv, K, V, grad_out, ou
             quantise_weight(*waiting)
 
         def transpose_tokens(j):
+            i, row = divmod(j, TILES_PER_LOAD)
             grads = tok_stage.tile([P, 2, QD], BF16)
-            nc.vector.tensor_tensor(
-                out=grads[:],
-                in0=g_sb[j // TILES_PER_LOAD][:, j % TILES_PER_LOAD, :].unsqueeze(1).to_broadcast([P, 2, QD]),
-                in1=factor_sb[j // TILES_PER_LOAD][:, :, j % TILES_PER_LOAD, :],
-                op=mybir.AluOpType.mult,
-            )
+            for m in range(2):
+                nc.vector.tensor_tensor(
+                    out=grads[:, m, :].rearrange("p (u w e) -> p w u e", u=2, e=2),
+                    in0=g_sb[i][:, row, :].rearrange("p (w u e) -> p w u e", u=2, e=2),
+                    in1=factor_sb[i][m][:, row, :].rearrange("p (w u e) -> p w u e", u=2, e=2),
+                    op=mybir.AluOpType.mult,
+                )
             grad_words = grads[:].rearrange("p m k -> p (m k)").bitcast(F32)
             words_t = psum_t.tile([P, 2, 2, P], F32)
             for m in range(2):
                 for u in range(2):
-                    first = 2 * m * P + u
-                    last = 2 * (m + 1) * P
-                    nc.tensor.transpose(words_t[:, m, u, :], grad_words[:, first:last:2], identity[:])
+                    first = (2 * m + u) * P
+                    nc.tensor.transpose(words_t[:, m, u, :], grad_words[:, first : first + P], identity[:])
             tok_grouped = tok_stage.tile([P, 2 * P * PACK], BF16, align_bytes=64)
             nc.scalar.copy(
                 out=tok_grouped[:].bitcast(F32).rearrange("p (m r u) -> p m r u", m=2, u=2),
@@ -161,7 +168,9 @@ def tile_parallelretention_pa_v_kernel(tc, x, Wk, bk, Wv, bv, K, V, grad_out, ou
                     nc.vector.tensor_copy(out=out_sb[:, j, cols], in_=acc[:])
                 else:
                     nc.scalar.copy(out=out_sb[:, j, cols], in_=acc[:])
-            cols = slice(chunks[0] * CHUNK, (chunks[-1] + 1) * CHUNK)
+
+        def store(j, first, last):
+            cols = slice(first * CHUNK, (last + 1) * CHUNK)
             nc.sync.dma_start(out=out_rows[:, j, cols], in_=out_sb[:, j, cols])
 
         load_tokens(0)
@@ -178,11 +187,19 @@ def tile_parallelretention_pa_v_kernel(tc, x, Wk, bk, Wv, bv, K, V, grad_out, ou
         prepare_weights([(1, chunk) for chunk in first_chunks])
         for j in range(TILES):
             multiply(j, first_chunks)
+            store(j, first_chunks[0], first_chunks[-1])
             if j + AHEAD < TILES:
                 tok_grouped.append(transpose_tokens(j + AHEAD))
             if j + 1 < TILES:
                 quantise_tokens(j + 1, tok_grouped[j + 1])
         for chunk in range(CHUNKS_PER_GROUP, CHUNKS):
             prepare_weights([(m, chunk) for m in range(2)])
-            for j in range(TILES):
+            for j in range(BY_CHUNK):
                 multiply(j, [chunk])
+                if j < SINGLE:
+                    store(j, chunk, chunk)
+                elif chunk == CHUNKS - 1:
+                    store(j, CHUNKS_PER_GROUP, chunk)
+        for j in range(BY_CHUNK, TILES):
+            multiply(j, [CHUNKS_PER_GROUP, CHUNKS - 1])
+            store(j, CHUNKS_PER_GROUP, CHUNKS - 1)

@@ -16,8 +16,9 @@ QD = P * PACK
 TOKENS = 1024
 E = 2048
 TILES = TOKENS // P
-TILES_PER_LOAD = 2
-LOADS = TILES // TILES_PER_LOAD
+LOAD_TILES = (2, 3, 3)
+LOADS = len(LOAD_TILES)
+LOAD_AND_ROW = [(i, row) for i, n in enumerate(LOAD_TILES) for row in range(n)]
 CHUNK = 512
 GROUP = 1024
 GROUPS = E // GROUP
@@ -55,17 +56,18 @@ def tile_parallelretention_pa_v_kernel(tc, x, Wk, bk, Wv, bv, K, V, grad_out, ou
     with ExitStack() as ctx:
         keep = ctx.enter_context(tc.tile_pool(name="keep", bufs=1))
         w_stage = ctx.enter_context(tc.tile_pool(name="w_stage", bufs=4))
-        tok_stage = ctx.enter_context(tc.tile_pool(name="tok_stage", bufs=4))
+        tok_stage = ctx.enter_context(tc.tile_pool(name="tok_stage", bufs=6))
         psum_t = ctx.enter_context(tc.psum_pool(name="psum_t", bufs=2))
         psum_acc = ctx.enter_context(tc.psum_pool(name="psum_acc", bufs=6))
 
         identity = keep.tile([P, P], F32)
         make_identity(nc, identity[:])
 
-        g_sb = [keep.tile([P, TILES_PER_LOAD, QD], BF16, name="g_sb_%d" % i) for i in range(LOADS)]
+        g_first = keep.tile([P, LOAD_TILES[0], QD], BF16)
+        g_rest = keep.tile([P, TILES - LOAD_TILES[0], QD], BF16)
         factor_sb = [
-            [keep.tile([P, TILES_PER_LOAD, QD], F32, name="factor_sb_%d_%d" % (i, m)) for m in range(2)]
-            for i in range(LOADS)
+            [keep.tile([P, n, QD], F32, name="factor_sb_%d_%d" % (i, m)) for m in range(2)]
+            for i, n in enumerate(LOAD_TILES)
         ]
         w_raw = [
             [keep.tile([P, PACK, GROUP], BF16, name="w_raw_%d_%d" % (group, m)) for m in range(2)]
@@ -78,8 +80,12 @@ def tile_parallelretention_pa_v_kernel(tc, x, Wk, bk, Wv, bv, K, V, grad_out, ou
         out_sb = keep.tile([P, TILES, E], F32)
 
         def load_tokens(i):
-            js = slice(i * TILES_PER_LOAD, (i + 1) * TILES_PER_LOAD)
-            nc.sync.dma_start(out=g_sb[i][:], in_=g_rows[:, js, :])
+            first = sum(LOAD_TILES[:i])
+            js = slice(first, first + LOAD_TILES[i])
+            if i == 0:
+                nc.sync.dma_start(out=g_first[:], in_=g_rows[:, js, :])
+            elif i == 1:
+                nc.sync.dma_start(out=g_rest[:], in_=g_rows[:, first:, :])
             for m in range(2):
                 nc.sync.dma_start(out=factor_sb[i][m][:], in_=factor_rows[m][:, js, :])
 
@@ -121,12 +127,13 @@ def tile_parallelretention_pa_v_kernel(tc, x, Wk, bk, Wv, bv, K, V, grad_out, ou
             quantise_weight(*waiting)
 
         def transpose_tokens(j):
-            i, row = divmod(j, TILES_PER_LOAD)
+            i, row = LOAD_AND_ROW[j]
+            g_row = g_first[:, j, :] if i == 0 else g_rest[:, j - LOAD_TILES[0], :]
             grads = tok_stage.tile([P, 2, QD], BF16)
             for m in range(2):
                 nc.vector.tensor_tensor(
                     out=grads[:, m, :].rearrange("p (u w e) -> p w u e", u=2, e=2),
-                    in0=g_sb[i][:, row, :].rearrange("p (w u e) -> p w u e", u=2, e=2),
+                    in0=g_row.rearrange("p (w u e) -> p w u e", u=2, e=2),
                     in1=factor_sb[i][m][:, row, :].rearrange("p (w u e) -> p w u e", u=2, e=2),
                     op=mybir.AluOpType.mult,
                 )
@@ -164,7 +171,7 @@ def tile_parallelretention_pa_v_kernel(tc, x, Wk, bk, Wv, bv, K, V, grad_out, ou
                         start=(m == 0),
                         stop=(m == 1),
                     )
-                if chunk == CHUNKS - 1 and j % 2 == 1:
+                if chunk == CHUNKS - 1 and j % 2 == 0:
                     nc.vector.tensor_copy(out=out_sb[:, j, cols], in_=acc[:])
                 else:
                     nc.scalar.copy(out=out_sb[:, j, cols], in_=acc[:])

from contextlib import ExitStack

import concourse.mybir as mybir
from concourse.masks import make_identity

F32 = mybir.dt.float32
BF16 = mybir.dt.bfloat16
U32 = mybir.dt.uint32
U8 = mybir.dt.uint8
E4M3X4 = mybir.dt.float8_e4m3fn_x4
E5M2X4 = mybir.dt.float8_e5m2_x4

P = 128
PACK = 4
QD = P * PACK
TOKENS = 1024
E = 2048
TILES = TOKENS // P
LOAD_TILES = (2, 3, 3)
LOADS = len(LOAD_TILES)
LOAD_AND_ROW = [(i, row) for i, n in enumerate(LOAD_TILES) for row in range(n)]
CHUNK = 512
GROUP = 1024
GROUPS = E // GROUP
CHUNKS_PER_GROUP = GROUP // CHUNK
CHUNKS = E // CHUNK
FIRST_GROUP_VECTOR_COLS = 320
BY_CHUNK = 6
SINGLE = 4
AHEAD = 2

FLOPS = 2 * 2 * TOKENS * QD * E
BYTES = 2 * QD * E * 2 + 2 * TOKENS * QD * 4 + TOKENS * QD * 2 + TOKENS * E * 4


def regrouped(dst, src):
    return (
        dst.rearrange("p (c i) t -> p c t i", i=4),
        src.rearrange("p t (c i) -> p c t i", i=4),
    )


def tile_parallelretention_pa_v_kernel(tc, x, Wk, bk, Wv, bv, K, V, grad_out, out):
    nc = tc.nc
    g_rows = grad_out.flatten_outer_dims().rearrange("(p j) k -> p j k", j=TILES)
    factor_rows = [
        V.flatten_outer_dims().rearrange("(p j) k -> p j k", j=TILES),
        K.flatten_outer_dims().rearrange("(p j) k -> p j k", j=TILES),
    ]
    out_rows = out.flatten_outer_dims().rearrange("(p j) e -> p j e", j=TILES)
    weight_rows = [
        Wk.rearrange("(p t) c -> p t c", t=PACK),
        Wv.rearrange("(p t) c -> p t c", t=PACK),
    ]

    with ExitStack() as ctx:
        keep = ctx.enter_context(tc.tile_pool(name="keep", bufs=1))
        w_stage = ctx.enter_context(tc.tile_pool(name="w_stage", bufs=4))
        tok_stage = ctx.enter_context(tc.tile_pool(name="tok_stage", bufs=6))
        psum_t = ctx.enter_context(tc.psum_pool(name="psum_t", bufs=2))
        psum_acc = ctx.enter_context(tc.psum_pool(name="psum_acc", bufs=6))

        identity = keep.tile([P, P], F32)
        make_identity(nc, identity[:])

        g_first = keep.tile([P, LOAD_TILES[0], QD], BF16)
        g_rest = keep.tile([P, TILES - LOAD_TILES[0], QD], BF16)
        factor_sb = [
            [keep.tile([P, n, QD], F32, name="factor_sb_%d_%d" % (i, m)) for m in range(2)]
            for i, n in enumerate(LOAD_TILES)
        ]
        w_raw = [
            [keep.tile([P, PACK, GROUP], BF16, name="w_raw_%d_%d" % (group, m)) for m in range(2)]
            for group in range(GROUPS)
        ]
        w_codes = keep.tile([P, 2, E], U32, align_bytes=64)
        w_scales = keep.tile([P, 2, E], U8, align_bytes=64)
        tok_codes = keep.tile([P, TILES, 2, P], U32, align_bytes=64)
        tok_scales = keep.tile([P, TILES, 2, P], U8, align_bytes=64)
        out_sb = keep.tile([P, TILES, E], F32)

        def load_tokens(i):
            first = sum(LOAD_TILES[:i])
            js = slice(first, first + LOAD_TILES[i])
            if i == 0:
                nc.sync.dma_start(out=g_first[:], in_=g_rows[:, js, :])
            elif i == 1:
                nc.sync.dma_start(out=g_rest[:], in_=g_rows[:, first:, :])
            for m in range(2):
                nc.sync.dma_start(out=factor_sb[i][m][:], in_=factor_rows[m][:, js, :])

        def load_weights(group):
            cols = slice(group * GROUP, (group + 1) * GROUP)
            for m in range(2):
                nc.sync.dma_start(out=w_raw[group][m][:], in_=weight_rows[m][:, :, cols])

        def regroup_weight(m, chunk):
            group = chunk // CHUNKS_PER_GROUP
            vector_cols = FIRST_GROUP_VECTOR_COLS if group == 0 else CHUNK
            raw = w_raw[group][m]
            c0 = (chunk % CHUNKS_PER_GROUP) * CHUNK
            c1 = c0 + vector_cols
            c2 = c0 + CHUNK
            w_grouped = w_stage.tile([P, CHUNK, PACK], BF16, align_bytes=64)
            dst, src = regrouped(w_grouped[:, 0:vector_cols, :], raw[:, :, c0:c1])
            nc.vector.tensor_copy(out=dst, in_=src)
            if vector_cols < CHUNK:
                dst, src = regrouped(w_grouped[:, vector_cols:CHUNK, :], raw[:, :, c1:c2])
                nc.scalar.copy(out=dst, in_=src)
            return w_grouped

        def quantise_weight(m, chunk, w_grouped):
            cols = slice(chunk * CHUNK, (chunk + 1) * CHUNK)
            nc.vector.quantize_mx(
                out=w_codes[:, m, cols].bitcast(E4M3X4),
                scales=w_scales[:, m, cols],
                in_=w_grouped[:].rearrange("p c t -> p (c t)"),
            )

        def prepare_weights(pieces):
            waiting = None
            for m, chunk in pieces:
                w_grouped = regroup_weight(m, chunk)
                if waiting is not None:
                    quantise_weight(*waiting)
                waiting = (m, chunk, w_grouped)
            quantise_weight(*waiting)

        def transpose_tokens(j):
            i, row = LOAD_AND_ROW[j]
            g_row = g_first[:, j, :] if i == 0 else g_rest[:, j - LOAD_TILES[0], :]
            grads = tok_stage.tile([P, 2, QD], BF16)
            for m in range(2):
                nc.vector.tensor_tensor(
                    out=grads[:, m, :].rearrange("p (u w e) -> p w u e", u=2, e=2),
                    in0=g_row.rearrange("p (w u e) -> p w u e", u=2, e=2),
                    in1=factor_sb[i][m][:, row, :].rearrange("p (w u e) -> p w u e", u=2, e=2),
                    op=mybir.AluOpType.mult,
                )
            grad_words = grads[:].rearrange("p m k -> p (m k)").bitcast(F32)
            words_t = psum_t.tile([P, 2, 2, P], F32)
            for m in range(2):
                for u in range(2):
                    first = (2 * m + u) * P
                    nc.tensor.transpose(words_t[:, m, u, :], grad_words[:, first : first + P], identity[:])
            tok_grouped = tok_stage.tile([P, 2 * P * PACK], BF16, align_bytes=64)
            nc.scalar.copy(
                out=tok_grouped[:].bitcast(F32).rearrange("p (m r u) -> p m r u", m=2, u=2),
                in_=words_t[:].rearrange("p m u r -> p m r u"),
            )
            return tok_grouped

        def quantise_tokens(j, tok_grouped):
            nc.vector.quantize_mx(
                out=tok_codes[:, j, :, :].rearrange("p m r -> p (m r)").bitcast(E5M2X4),
                scales=tok_scales[:, j, :, :].rearrange("p m r -> p (m r)"),
                in_=tok_grouped[:],
            )

        def multiply(j, chunks):
            for chunk in chunks:
                cols = slice(chunk * CHUNK, (chunk + 1) * CHUNK)
                acc = psum_acc.tile([P, CHUNK], F32)
                for m in range(2):
                    nc.tensor.matmul_mx(
                        out=acc[:],
                        lhsT=tok_codes[:, j, m, :].bitcast(E5M2X4),
                        lhsT_scale=tok_scales[:, j, m, :],
                        rhs=w_codes[:, m, cols].bitcast(E4M3X4),
                        rhs_scale=w_scales[:, m, cols],
                        start=(m == 0),
                        stop=(m == 1),
                    )
                if chunk == CHUNKS - 1 and j % 2 == 0:
                    nc.vector.tensor_copy(out=out_sb[:, j, cols], in_=acc[:])
                else:
                    nc.scalar.copy(out=out_sb[:, j, cols], in_=acc[:])

        def store(j, first, last):
            cols = slice(first * CHUNK, (last + 1) * CHUNK)
            nc.sync.dma_start(out=out_rows[:, j, cols], in_=out_sb[:, j, cols])

        load_tokens(0)
        load_weights(0)
        for i in range(1, LOADS):
            load_tokens(i)
        for group in range(1, GROUPS):
            load_weights(group)

        first_chunks = list(range(CHUNKS_PER_GROUP))
        tok_grouped = [transpose_tokens(j) for j in range(AHEAD)]
        prepare_weights([(0, chunk) for chunk in first_chunks])
        quantise_tokens(0, tok_grouped[0])
        prepare_weights([(1, chunk) for chunk in first_chunks])
        for j in range(TILES):
            multiply(j, first_chunks)
            store(j, first_chunks[0], first_chunks[-1])
            if j + AHEAD < TILES:
                tok_grouped.append(transpose_tokens(j + AHEAD))
            if j + 1 < TILES:
                quantise_tokens(j + 1, tok_grouped[j + 1])
        for chunk in range(CHUNKS_PER_GROUP, CHUNKS):
            prepare_weights([(m, chunk) for m in range(2)])
            for j in range(BY_CHUNK):
                multiply(j, [chunk])
                if j < SINGLE:
                    store(j, chunk, chunk)
                elif chunk == CHUNKS - 1:
                    store(j, CHUNKS_PER_GROUP, chunk)
        for j in range(BY_CHUNK, TILES):
            multiply(j, [CHUNKS_PER_GROUP, CHUNKS - 1])
            store(j, CHUNKS_PER_GROUP, CHUNKS - 1)
